import numpy as np
import ml_dtypes


def mxq(x, axis, fmt="e4m3"):
    dtype, down = {"e4m3": (ml_dtypes.float8_e4m3fn, 7), "e5m2": (ml_dtypes.float8_e5m2, 14)}[fmt]
    v = np.moveaxis(np.asarray(x, np.float32).astype(ml_dtypes.bfloat16).astype(np.float64), axis, -1)
    blocks = v.reshape(v.shape[:-1] + (-1, 32))
    amax = np.abs(blocks).max(-1, keepdims=True)
    byte = np.maximum(np.where(amax > 0, np.frexp(amax)[1] - 1 + 127, 0) - down, 1)
    scale = np.exp2(byte - 127.0)
    codes = (blocks / scale).astype(np.float32).astype(dtype).astype(np.float64)
    return np.moveaxis((codes * scale).reshape(v.shape), -1, axis)


WIDE = False


def mx_kscale(k):
    if not WIDE:
        return np.ones(k)
    levels = np.array([10, -10, 5, -5, 0])
    a = np.random.permutation(np.resize(levels, k // 512 * 4)).reshape(k // 512, 4)
    idx = np.arange(k)
    return np.exp2(a[idx // 512, idx % 128 // 32])


BF16 = ml_dtypes.bfloat16


def bf(x):
    return np.asarray(x, np.float32).astype(BF16)


def f64(x):
    return np.asarray(x).astype(np.float64)


E2M1 = np.array([0.0, 0.5, 1.0, 1.5, 2.0, 3.0, 4.0, 6.0, -0.0, -0.5, -1.0, -1.5, -2.0, -3.0, -4.0, -6.0])


def pack_weight(w, fmt):
    k, n = w.shape
    w = f64(bf(w)).reshape(k // 32, 32, n)
    amax = np.abs(w).max(1)
    if fmt == "e4m3":
        byte = np.frexp(amax)[1] - 1 + 127 - 7
    else:
        mant, ex = np.frexp(amax / 6.0)
        byte = np.where(mant > 0.5, ex, ex - 1) + 127
    byte = np.clip(np.where(amax > 0, byte, 1), 1, 254)
    scaled = (w * np.exp2(127.0 - byte)[:, None, :]).reshape(k, n).astype(np.float32)
    by_word = np.ascontiguousarray(scaled.reshape(k // 512, 128, 4, n).transpose(0, 1, 3, 2))
    if fmt == "e4m3":
        words = by_word.astype(ml_dtypes.float8_e4m3fn).view(np.uint8)
    else:
        c = by_word.astype(ml_dtypes.float4_e2m1fn).view(np.uint8) & 0xF
        words = c[..., 0::2] | (c[..., 1::2] << 4)
    return np.ascontiguousarray(words), np.ascontiguousarray(byte.astype(np.uint8).reshape(k // 512, 16, n))


def unpack_weight(words, scales, fmt):
    g, p, n, _ = words.shape
    if fmt == "e4m3":
        vals = np.ascontiguousarray(words).view(ml_dtypes.float8_e4m3fn).astype(np.float64)
    else:
        nib = np.empty((g, p, n, 4), np.uint8)
        nib[..., 0::2] = words & 0xF
        nib[..., 1::2] = words >> 4
        vals = E2M1[nib]
    vals = vals * np.repeat(np.exp2(scales.astype(np.float64) - 127.0), 8, axis=1)[..., None]
    return vals.transpose(0, 1, 3, 2).reshape(g * 512, n)


B, S, N, D = 2, 64, 4096, 4096


def setup_inputs():
    s = mx_kscale(N)
    input_numeric = bf(np.random.standard_normal((B, S, 1)))
    proj_w = bf(np.random.standard_normal((N, 1)))
    proj_b = bf(np.random.standard_normal(N) + np.log(s))
    words, scales = pack_weight(np.random.standard_normal((N, D)) * 0.15 * np.sqrt(N) * np.mean(s) / s[:, None], "e4m3")
    return {"input_numeric": input_numeric,
            "proj_w": proj_w,
            "proj_b": proj_b,
            "emb_table_words": words,
            "emb_table_scales": scales}


def reference(input_numeric, proj_w, proj_b, emb_table_words, emb_table_scales):
    logits = f64(input_numeric) * f64(proj_w)[:, 0] + f64(proj_b)
    e = np.exp(logits - logits.max(-1, keepdims=True))
    weights = e / e.sum(-1, keepdims=True)
    return mxq(weights, 2, "e4m3") @ unpack_weight(emb_table_words, emb_table_scales, "e4m3")

@@ -1,0 +1,170 @@
+from contextlib import ExitStack
+
+import concourse.mybir as mybir
+from concourse.masks import make_identity
+
+F32 = mybir.dt.float32
+BF16 = mybir.dt.bfloat16
+I32 = mybir.dt.int32
+U8 = mybir.dt.uint8
+FP8X4 = mybir.dt.float8_e4m3fn_x4
+ACT = mybir.ActivationFunctionType
+ALU = mybir.AluOpType
+AX = mybir.AxisListType
+
+P = 128
+PACK = 4
+K_PASS = P * PACK
+N_EMB = 4096
+D_OUT = 4096
+PASSES = N_EMB // K_PASS
+BANK = 512
+BANKS = D_OUT // BANK
+PLANES_PER_TILE = 4
+LAST_CHUNKS = 4
+
+FLOPS = 2 * P * N_EMB * D_OUT
+
+
+def tile_softembedding_w_kernel(
+    tc, input_numeric, proj_w, proj_b, emb_table_words, emb_table_scales, out
+):
+    nc = tc.nc
+    with ExitStack() as ctx:
+        keep = ctx.enter_context(tc.tile_pool(name="keep", bufs=1))
+        psum = ctx.enter_context(tc.psum_pool(name="psum", bufs=1))
+
+        planes = [
+            keep.tile([P, D_OUT], U8, name="planes%d" % s, align_bytes=64)
+            for s in range(PASSES // PLANES_PER_TILE)
+        ]
+        words = [
+            keep.tile([P, D_OUT], I32, name="words%d" % g, align_bytes=64)
+            for g in range(PASSES)
+        ]
+        x_ones = keep.tile([P, P], BF16, name="x_ones")
+        wb_rows = keep.tile([P, N_EMB], BF16, name="wb_rows")
+        warm = keep.tile([P, 1], F32, name="warm")
+
+        for s in range(len(planes)):
+            nc.vector.memset(planes[s][:].bitcast(I32), 0)
+        nc.vector.memset(warm[:], 0.0)
+        nc.vector.memset(x_ones[:], 1.0)
+        nc.vector.memset(wb_rows[:].bitcast(I32), 0)
+
+        nc.scalar.activation(out=warm[:], in_=warm[:], func=ACT.Exp)
+
+        nc.scalar.dma_start(out=x_ones[0:1, :], in_=input_numeric.rearrange("b s o -> o (b s)"))
+        nc.scalar.dma_start(out=wb_rows[0:1, :], in_=proj_w.rearrange("n o -> o n"))
+        nc.scalar.dma_start(out=wb_rows[1:2, :], in_=proj_b.rearrange("(o n) -> o n", o=1))
+
+        for s in range(len(planes)):
+            for quad in range(4):
+                nc.sync.dma_start(
+                    out=planes[s][32 * quad : 32 * quad + 16, :].bitcast(I32),
+                    in_=emb_table_scales[
+                        PLANES_PER_TILE * s : PLANES_PER_TILE * (s + 1), 4 * quad : 4 * quad + 4, :
+                    ].bitcast(I32),
+                )
+        chunk = D_OUT // LAST_CHUNKS
+        for g in range(PASSES):
+            src = emb_table_words[g].rearrange("p n t -> p (n t)").bitcast(I32)
+            if g < PASSES - 1:
+                nc.sync.dma_start(out=words[g][:], in_=src)
+            else:
+                for c in range(LAST_CHUNKS):
+                    cols = slice(c * chunk, (c + 1) * chunk)
+                    nc.sync.dma_start(out=words[g][:, cols], in_=src[:, cols])
+
+        ident = keep.tile([P, P], BF16, name="ident")
+        make_identity(nc, ident[:])
+
+        part_max = keep.tile([P, BANKS], F32, name="part_max")
+        logits = []
+        for j in range(PASSES):
+            lg = psum.tile([P, BANK], F32, name="logits%d" % j, tag="bank%d" % j)
+            nc.tensor.matmul(
+                out=lg[:], lhsT=x_ones[:], rhs=wb_rows[:, j * BANK : (j + 1) * BANK], start=True, stop=True
+            )
+            nc.vector.tensor_reduce(out=part_max[:, j : j + 1], in_=lg[:], axis=AX.X, op=ALU.max)
+            logits.append(lg)
+        top = keep.tile([P, 1], F32, name="top")
+        neg_top = keep.tile([P, 1], F32, name="neg_top")
+        nc.vector.tensor_reduce(out=top[:], in_=part_max[:], axis=AX.X, op=ALU.max)
+        nc.vector.tensor_scalar(out=neg_top[:], in0=top[:], scalar1=-1.0, scalar2=None, op0=ALU.mult)
+
+        exps = keep.tile([P, N_EMB], F32, name="exps")
+        part_sum = keep.tile([P, BANKS], F32, name="part_sum")
+        for j in range(PASSES):
+            nc.scalar.activation(
+                out=exps[:, j * BANK : (j + 1) * BANK],
+                in_=logits[j][:],
+                func=ACT.Exp,
+                bias=neg_top[:, 0:1],
+                scale=1.0,
+                accum_out=part_sum[:, j : j + 1],
+            )
+        total = keep.tile([P, 1], F32, name="total")
+        inv_total = keep.tile([P, 1], F32, name="inv_total")
+        nc.vector.tensor_reduce(out=total[:], in_=part_sum[:], axis=AX.X, op=ALU.add)
+        nc.vector.reciprocal(out=inv_total[:], in_=total[:])
+
+        soft = keep.tile([P, PASSES, P, PACK], BF16, name="soft")
+        grouped = keep.tile([P, PASSES, P, PACK], BF16, name="grouped", align_bytes=64)
+        codes = keep.tile([P, PASSES, P], I32, name="codes", align_bytes=64)
+        code_scales = keep.tile([P, PASSES, P], U8, name="code_scales", align_bytes=64)
+        for g in range(PASSES):
+            nc.vector.tensor_scalar(
+                out=soft[:, g].rearrange("m p t -> m (p t)"),
+                in0=exps[:, g * K_PASS : (g + 1) * K_PASS],
+                scalar1=inv_total[:, 0:1],
+                scalar2=None,
+                op0=ALU.mult,
+            )
+        flipped = []
+        for g in range(PASSES):
+            fl = psum.tile([P, PACK, P], BF16, name="flipped%d" % g, tag="bank%d" % g)
+            for t in range(PACK):
+                nc.tensor.transpose(fl[:, t, :], soft[:, g, :, t], ident[:])
+            flipped.append(fl)
+        for g in range(PASSES):
+            src = flipped[g][:].rearrange("p t m -> p m t")
+            if g % 2 == 0:
+                nc.vector.tensor_copy(out=grouped[:, g], in_=src)
+            else:
+                nc.scalar.copy(out=grouped[:, g], in_=src)
+        for g in range(PASSES):
+            nc.vector.quantize_mx(
+                out=codes[:, g, :].bitcast(FP8X4),
+                scales=code_scales[:, g, :],
+                in_=grouped[:, g].rearrange("p m t -> p (m t)"),
+            )
+
+        acc = [psum.tile([P, BANK], F32, name="acc%d" % j, tag="bank%d" % j) for j in range(BANKS)]
+        for g in range(PASSES):
+            plane = planes[g // PLANES_PER_TILE]
+            first_row = 4 * (g % PLANES_PER_TILE)
+            for j in range(BANKS):
+                cols = slice(j * BANK, (j + 1) * BANK)
+                nc.tensor.matmul_mx(
+                    out=acc[j][:],
+                    lhsT=codes[:, g, :].bitcast(FP8X4),
+                    lhsT_scale=code_scales[:, g, :],
+                    rhs=words[g][:, cols].bitcast(FP8X4),
+                    rhs_scale=plane[first_row:P, cols],
+                    start=(g == 0),
+                    stop=(g == PASSES - 1),
+                )
+
+        result = keep.tile([P, D_OUT], F32, name="result")
+        out_rows = out.rearrange("b s d -> (b s) d")
+        banks_per_chunk = BANKS // LAST_CHUNKS
+        for c in range(LAST_CHUNKS):
+            for j in range(c * banks_per_chunk, (c + 1) * banks_per_chunk):
+                cols = slice(j * BANK, (j + 1) * BANK)
+                if j % 2 == 0:
+                    nc.vector.tensor_copy(out=result[:, cols], in_=acc[j][:])
+                else:
+                    nc.scalar.copy(out=result[:, cols], in_=acc[j][:])
+            cols = slice(c * chunk, (c + 1) * chunk)
+            nc.sync.dma_start(out=out_rows[:, cols], in_=result[:, cols])

@@ -22,6 +22,7 @@ BANK = 512
 BANKS = D_OUT // BANK
 PLANES_PER_TILE = 4
 LAST_CHUNKS = 4
+HALVES = 2
 
 FLOPS = 2 * P * N_EMB * D_OUT
 
@@ -33,6 +34,7 @@ def tile_softembedding_w_kernel(
     with ExitStack() as ctx:
         keep = ctx.enter_context(tc.tile_pool(name="keep", bufs=1))
         psum = ctx.enter_context(tc.psum_pool(name="psum", bufs=1))
+        ctx.enter_context(tc.manual_schedule())
 
         planes = [
             keep.tile([P, D_OUT], U8, name="planes%d" % s, align_bytes=64)
@@ -76,63 +78,66 @@ def tile_softembedding_w_kernel(
                     cols = slice(c * chunk, (c + 1) * chunk)
                     nc.sync.dma_start(out=words[g][:, cols], in_=src[:, cols])
 
-        ident = keep.tile([P, P], BF16, name="ident")
+        ident = keep.tile([P, P], F32, name="ident")
         make_identity(nc, ident[:])
 
-        part_max = keep.tile([P, BANKS], F32, name="part_max")
-        logits = []
-        for j in range(PASSES):
-            lg = psum.tile([P, BANK], F32, name="logits%d" % j, tag="bank%d" % j)
-            nc.tensor.matmul(
-                out=lg[:], lhsT=x_ones[:], rhs=wb_rows[:, j * BANK : (j + 1) * BANK], start=True, stop=True
-            )
-            nc.vector.tensor_reduce(out=part_max[:, j : j + 1], in_=lg[:], axis=AX.X, op=ALU.max)
-            logits.append(lg)
-        top = keep.tile([P, 1], F32, name="top")
-        neg_top = keep.tile([P, 1], F32, name="neg_top")
-        nc.vector.tensor_reduce(out=top[:], in_=part_max[:], axis=AX.X, op=ALU.max)
-        nc.vector.tensor_scalar(out=neg_top[:], in0=top[:], scalar1=-1.0, scalar2=None, op0=ALU.mult)
-
-        exps = keep.tile([P, N_EMB], F32, name="exps")
+        neg_max = keep.tile([P, BANKS], F32, name="neg_max")
         part_sum = keep.tile([P, BANKS], F32, name="part_sum")
-        for j in range(PASSES):
-            nc.scalar.activation(
-                out=exps[:, j * BANK : (j + 1) * BANK],
-                in_=logits[j][:],
-                func=ACT.Exp,
-                bias=neg_top[:, 0:1],
-                scale=1.0,
-                accum_out=part_sum[:, j : j + 1],
+        exps = keep.tile([P, N_EMB], F32, name="exps")
+        for g in range(PASSES):
+            lg = psum.tile([P, BANK], F32, name="logits%d" % g, tag="bank%d" % g)
+            nc.tensor.matmul(
+                out=lg[:].rearrange("m (u p e) -> m p u e", u=HALVES, e=2),
+                lhsT=x_ones[:],
+                rhs=wb_rows[:, g * K_PASS : (g + 1) * K_PASS].rearrange("k (p u e) -> k p u e", u=HALVES, e=2),
+                start=True,
+                stop=True,
             )
+            nc.vector.tensor_reduce(out=neg_max[:, g : g + 1], in_=lg[:], axis=AX.X, op=ALU.max, negate=True)
+            nc.scalar.activation(
+                out=exps[:, g * K_PASS : (g + 1) * K_PASS],
+                in_=lg[:],
+                func=ACT.Exp,
+                bias=neg_max[:, g : g + 1],
+                scale=1.0,
+                accum_out=part_sum[:, g : g + 1],
+            )
+
+        neg_top = keep.tile([P, 1], F32, name="neg_top")
+        factor = keep.tile([P, BANKS], F32, name="factor")
+        weighted = keep.tile([P, BANKS], F32, name="weighted")
         total = keep.tile([P, 1], F32, name="total")
         inv_total = keep.tile([P, 1], F32, name="inv_total")
-        nc.vector.tensor_reduce(out=total[:], in_=part_sum[:], axis=AX.X, op=ALU.add)
+        gain = keep.tile([P, BANKS], F32, name="gain")
+        nc.vector.tensor_reduce(out=neg_top[:], in_=neg_max[:], axis=AX.X, op=ALU.min)
+        nc.scalar.activation(out=factor[:], in_=neg_max[:], func=ACT.Exp, bias=neg_top[:, 0:1], scale=-1.0)
+        nc.vector.scalar_tensor_tensor(
+            out=weighted[:], in0=factor[:], scalar=1.0, in1=part_sum[:], op0=ALU.mult, op1=ALU.mult, accum_out=total[:]
+        )
         nc.vector.reciprocal(out=inv_total[:], in_=total[:])
+        nc.vector.tensor_scalar(out=gain[:], in0=factor[:], scalar1=inv_total[:, 0:1], scalar2=None, op0=ALU.mult)
 
-        soft = keep.tile([P, PASSES, P, PACK], BF16, name="soft")
+        soft = keep.tile([P, N_EMB], BF16, name="soft")
         grouped = keep.tile([P, PASSES, P, PACK], BF16, name="grouped", align_bytes=64)
         codes = keep.tile([P, PASSES, P], I32, name="codes", align_bytes=64)
         code_scales = keep.tile([P, PASSES, P], U8, name="code_scales", align_bytes=64)
+        soft_words = soft[:].bitcast(F32)
         for g in range(PASSES):
             nc.vector.tensor_scalar(
-                out=soft[:, g].rearrange("m p t -> m (p t)"),
+                out=soft[:, g * K_PASS : (g + 1) * K_PASS],
                 in0=exps[:, g * K_PASS : (g + 1) * K_PASS],
-                scalar1=inv_total[:, 0:1],
+                scalar1=gain[:, g : g + 1],
                 scalar2=None,
                 op0=ALU.mult,
             )
-        flipped = []
-        for g in range(PASSES):
-            fl = psum.tile([P, PACK, P], BF16, name="flipped%d" % g, tag="bank%d" % g)
-            for t in range(PACK):
-                nc.tensor.transpose(fl[:, t, :], soft[:, g, :, t], ident[:])
-            flipped.append(fl)
-        for g in range(PASSES):
-            src = flipped[g][:].rearrange("p t m -> p m t")
-            if g % 2 == 0:
-                nc.vector.tensor_copy(out=grouped[:, g], in_=src)
-            else:
-                nc.scalar.copy(out=grouped[:, g], in_=src)
+            fl = psum.tile([P, HALVES, P], F32, name="flipped%d" % g, tag="bank%d" % g)
+            for u in range(HALVES):
+                first = (g * HALVES + u) * P
+                nc.tensor.transpose(fl[:, u, :], soft_words[:, first : first + P], ident[:])
+            nc.scalar.copy(
+                out=grouped[:, g].rearrange("p m t -> p (m t)").bitcast(F32).rearrange("p (m u) -> p m u", u=HALVES),
+                in_=fl[:].rearrange("p u m -> p m u"),
+            )
         for g in range(PASSES):
             nc.vector.quantize_mx(
                 out=codes[:, g, :].bitcast(FP8X4),

@@ -48,17 +48,13 @@ def tile_softembedding_w_kernel(
         wb_rows = keep.tile([P, N_EMB], BF16, name="wb_rows")
         warm = keep.tile([P, 1], F32, name="warm")
 
+        nc.gpsimd.memset(warm[:], 0.0)
         for s in range(len(planes)):
             nc.vector.memset(planes[s][:].bitcast(I32), 0)
-        nc.vector.memset(warm[:], 0.0)
         nc.vector.memset(x_ones[:], 1.0)
         nc.vector.memset(wb_rows[:].bitcast(I32), 0)
 
         nc.scalar.activation(out=warm[:], in_=warm[:], func=ACT.Exp)
-
-        nc.scalar.dma_start(out=x_ones[0:1, :], in_=input_numeric.rearrange("b s o -> o (b s)"))
-        nc.scalar.dma_start(out=wb_rows[0:1, :], in_=proj_w.rearrange("n o -> o n"))
-        nc.scalar.dma_start(out=wb_rows[1:2, :], in_=proj_b.rearrange("(o n) -> o n", o=1))
 
         for s in range(len(planes)):
             for quad in range(4):
@@ -68,6 +64,9 @@ def tile_softembedding_w_kernel(
                         PLANES_PER_TILE * s : PLANES_PER_TILE * (s + 1), 4 * quad : 4 * quad + 4, :
                     ].bitcast(I32),
                 )
+        nc.sync.dma_start(out=x_ones[0:1, :], in_=input_numeric.rearrange("b s o -> o (b s)"))
+        nc.sync.dma_start(out=wb_rows[0:1, :], in_=proj_w.rearrange("n o -> o n"))
+        nc.sync.dma_start(out=wb_rows[1:2, :], in_=proj_b.rearrange("(o n) -> o n", o=1))
         chunk = D_OUT // LAST_CHUNKS
         for g in range(PASSES):
             src = emb_table_words[g].rearrange("p n t -> p (n t)").bitcast(I32)

@@ -49,33 +49,35 @@ def tile_softembedding_w_kernel(
         warm = keep.tile([P, 1], F32, name="warm")
 
         nc.gpsimd.memset(warm[:], 0.0)
-        for s in range(len(planes)):
-            nc.vector.memset(planes[s][:].bitcast(I32), 0)
         nc.vector.memset(x_ones[:], 1.0)
         nc.vector.memset(wb_rows[:].bitcast(I32), 0)
+        for s in range(len(planes)):
+            nc.vector.memset(planes[s][:].bitcast(I32), 0)
 
         nc.scalar.activation(out=warm[:], in_=warm[:], func=ACT.Exp)
 
-        for s in range(len(planes)):
-            for quad in range(4):
-                nc.sync.dma_start(
-                    out=planes[s][32 * quad : 32 * quad + 16, :].bitcast(I32),
-                    in_=emb_table_scales[
-                        PLANES_PER_TILE * s : PLANES_PER_TILE * (s + 1), 4 * quad : 4 * quad + 4, :
-                    ].bitcast(I32),
-                )
+        def load_words(g, cols):
+            src = emb_table_words[g].rearrange("p n t -> p (n t)").bitcast(I32)
+            nc.sync.dma_start(out=words[g][:, cols], in_=src[:, cols])
+
+        load_words(0, slice(0, D_OUT))
         nc.sync.dma_start(out=x_ones[0:1, :], in_=input_numeric.rearrange("b s o -> o (b s)"))
         nc.sync.dma_start(out=wb_rows[0:1, :], in_=proj_w.rearrange("n o -> o n"))
         nc.sync.dma_start(out=wb_rows[1:2, :], in_=proj_b.rearrange("(o n) -> o n", o=1))
+        for quads in ((2, 3), (0, 1)):
+            for s in range(len(planes)):
+                for quad in quads:
+                    nc.sync.dma_start(
+                        out=planes[s][32 * quad : 32 * quad + 16, :].bitcast(I32),
+                        in_=emb_table_scales[
+                            PLANES_PER_TILE * s : PLANES_PER_TILE * (s + 1), 4 * quad : 4 * quad + 4, :
+                        ].bitcast(I32),
+                    )
         chunk = D_OUT // LAST_CHUNKS
-        for g in range(PASSES):
-            src = emb_table_words[g].rearrange("p n t -> p (n t)").bitcast(I32)
-            if g < PASSES - 1:
-                nc.sync.dma_start(out=words[g][:], in_=src)
-            else:
-                for c in range(LAST_CHUNKS):
-                    cols = slice(c * chunk, (c + 1) * chunk)
-                    nc.sync.dma_start(out=words[g][:, cols], in_=src[:, cols])
+        for g in range(1, PASSES - 1):
+            load_words(g, slice(0, D_OUT))
+        for c in range(LAST_CHUNKS):
+            load_words(PASSES - 1, slice(c * chunk, (c + 1) * chunk))
 
         ident = keep.tile([P, P], F32, name="ident")
         make_identity(nc, ident[:])

@@ -74,8 +74,10 @@ def tile_softembedding_w_kernel(
                         ].bitcast(I32),
                     )
         chunk = D_OUT // LAST_CHUNKS
-        for g in range(1, PASSES - 1):
+        for g in range(1, PASSES - 2):
             load_words(g, slice(0, D_OUT))
+        for half in range(2):
+            load_words(PASSES - 2, slice(half * D_OUT // 2, (half + 1) * D_OUT // 2))
         for c in range(LAST_CHUNKS):
             load_words(PASSES - 1, slice(c * chunk, (c + 1) * chunk))
 

from contextlib import ExitStack

import concourse.mybir as mybir
from concourse.masks import make_identity

F32 = mybir.dt.float32
BF16 = mybir.dt.bfloat16
I32 = mybir.dt.int32
U8 = mybir.dt.uint8
FP8X4 = mybir.dt.float8_e4m3fn_x4
ACT = mybir.ActivationFunctionType
ALU = mybir.AluOpType
AX = mybir.AxisListType

P = 128
PACK = 4
K_PASS = P * PACK
N_EMB = 4096
D_OUT = 4096
PASSES = N_EMB // K_PASS
BANK = 512
BANKS = D_OUT // BANK
PLANES_PER_TILE = 4
LAST_CHUNKS = 4
HALVES = 2

FLOPS = 2 * P * N_EMB * D_OUT


def tile_softembedding_w_kernel(
    tc, input_numeric, proj_w, proj_b, emb_table_words, emb_table_scales, out
):
    nc = tc.nc
    with ExitStack() as ctx:
        keep = ctx.enter_context(tc.tile_pool(name="keep", bufs=1))
        psum = ctx.enter_context(tc.psum_pool(name="psum", bufs=1))
        ctx.enter_context(tc.manual_schedule())

        planes = [
            keep.tile([P, D_OUT], U8, name="planes%d" % s, align_bytes=64)
            for s in range(PASSES // PLANES_PER_TILE)
        ]
        words = [
            keep.tile([P, D_OUT], I32, name="words%d" % g, align_bytes=64)
            for g in range(PASSES)
        ]
        x_ones = keep.tile([P, P], BF16, name="x_ones")
        wb_rows = keep.tile([P, N_EMB], BF16, name="wb_rows")
        warm = keep.tile([P, 1], F32, name="warm")

        nc.gpsimd.memset(warm[:], 0.0)
        nc.vector.memset(x_ones[:], 1.0)
        nc.vector.memset(wb_rows[:].bitcast(I32), 0)
        for s in range(len(planes)):
            nc.vector.memset(planes[s][:].bitcast(I32), 0)

        nc.scalar.activation(out=warm[:], in_=warm[:], func=ACT.Exp)

        def load_words(g, cols):
            src = emb_table_words[g].rearrange("p n t -> p (n t)").bitcast(I32)
            nc.sync.dma_start(out=words[g][:, cols], in_=src[:, cols])

        load_words(0, slice(0, D_OUT))
        nc.sync.dma_start(out=x_ones[0:1, :], in_=input_numeric.rearrange("b s o -> o (b s)"))
        nc.sync.dma_start(out=wb_rows[0:1, :], in_=proj_w.rearrange("n o -> o n"))
        nc.sync.dma_start(out=wb_rows[1:2, :], in_=proj_b.rearrange("(o n) -> o n", o=1))
        for quads in ((2, 3), (0, 1)):
            for s in range(len(planes)):
                for quad in quads:
                    nc.sync.dma_start(
                        out=planes[s][32 * quad : 32 * quad + 16, :].bitcast(I32),
                        in_=emb_table_scales[
                            PLANES_PER_TILE * s : PLANES_PER_TILE * (s + 1), 4 * quad : 4 * quad + 4, :
                        ].bitcast(I32),
                    )
        chunk = D_OUT // LAST_CHUNKS
        for g in range(1, PASSES - 2):
            load_words(g, slice(0, D_OUT))
        for half in range(2):
            load_words(PASSES - 2, slice(half * D_OUT // 2, (half + 1) * D_OUT // 2))
        for c in range(LAST_CHUNKS):
            load_words(PASSES - 1, slice(c * chunk, (c + 1) * chunk))

        ident = keep.tile([P, P], F32, name="ident")
        make_identity(nc, ident[:])

        neg_max = keep.tile([P, BANKS], F32, name="neg_max")
        part_sum = keep.tile([P, BANKS], F32, name="part_sum")
        exps = keep.tile([P, N_EMB], F32, name="exps")
        for g in range(PASSES):
            lg = psum.tile([P, BANK], F32, name="logits%d" % g, tag="bank%d" % g)
            nc.tensor.matmul(
                out=lg[:].rearrange("m (u p e) -> m p u e", u=HALVES, e=2),
                lhsT=x_ones[:],
                rhs=wb_rows[:, g * K_PASS : (g + 1) * K_PASS].rearrange("k (p u e) -> k p u e", u=HALVES, e=2),
                start=True,
                stop=True,
            )
            nc.vector.tensor_reduce(out=neg_max[:, g : g + 1], in_=lg[:], axis=AX.X, op=ALU.max, negate=True)
            nc.scalar.activation(
                out=exps[:, g * K_PASS : (g + 1) * K_PASS],
                in_=lg[:],
                func=ACT.Exp,
                bias=neg_max[:, g : g + 1],
                scale=1.0,
                accum_out=part_sum[:, g : g + 1],
            )

        neg_top = keep.tile([P, 1], F32, name="neg_top")
        factor = keep.tile([P, BANKS], F32, name="factor")
        weighted = keep.tile([P, BANKS], F32, name="weighted")
        total = keep.tile([P, 1], F32, name="total")
        inv_total = keep.tile([P, 1], F32, name="inv_total")
        gain = keep.tile([P, BANKS], F32, name="gain")
        nc.vector.tensor_reduce(out=neg_top[:], in_=neg_max[:], axis=AX.X, op=ALU.min)
        nc.scalar.activation(out=factor[:], in_=neg_max[:], func=ACT.Exp, bias=neg_top[:, 0:1], scale=-1.0)
        nc.vector.scalar_tensor_tensor(
            out=weighted[:], in0=factor[:], scalar=1.0, in1=part_sum[:], op0=ALU.mult, op1=ALU.mult, accum_out=total[:]
        )
        nc.vector.reciprocal(out=inv_total[:], in_=total[:])
        nc.vector.tensor_scalar(out=gain[:], in0=factor[:], scalar1=inv_total[:, 0:1], scalar2=None, op0=ALU.mult)

        soft = keep.tile([P, N_EMB], BF16, name="soft")
        grouped = keep.tile([P, PASSES, P, PACK], BF16, name="grouped", align_bytes=64)
        codes = keep.tile([P, PASSES, P], I32, name="codes", align_bytes=64)
        code_scales = keep.tile([P, PASSES, P], U8, name="code_scales", align_bytes=64)
        soft_words = soft[:].bitcast(F32)
        for g in range(PASSES):
            nc.vector.tensor_scalar(
                out=soft[:, g * K_PASS : (g + 1) * K_PASS],
                in0=exps[:, g * K_PASS : (g + 1) * K_PASS],
                scalar1=gain[:, g : g + 1],
                scalar2=None,
                op0=ALU.mult,
            )
            fl = psum.tile([P, HALVES, P], F32, name="flipped%d" % g, tag="bank%d" % g)
            for u in range(HALVES):
                first = (g * HALVES + u) * P
                nc.tensor.transpose(fl[:, u, :], soft_words[:, first : first + P], ident[:])
            nc.scalar.copy(
                out=grouped[:, g].rearrange("p m t -> p (m t)").bitcast(F32).rearrange("p (m u) -> p m u", u=HALVES),
                in_=fl[:].rearrange("p u m -> p m u"),
            )
        for g in range(PASSES):
            nc.vector.quantize_mx(
                out=codes[:, g, :].bitcast(FP8X4),
                scales=code_scales[:, g, :],
                in_=grouped[:, g].rearrange("p m t -> p (m t)"),
            )

        acc = [psum.tile([P, BANK], F32, name="acc%d" % j, tag="bank%d" % j) for j in range(BANKS)]
        for g in range(PASSES):
            plane = planes[g // PLANES_PER_TILE]
            first_row = 4 * (g % PLANES_PER_TILE)
            for j in range(BANKS):
                cols = slice(j * BANK, (j + 1) * BANK)
                nc.tensor.matmul_mx(
                    out=acc[j][:],
                    lhsT=codes[:, g, :].bitcast(FP8X4),
                    lhsT_scale=code_scales[:, g, :],
                    rhs=words[g][:, cols].bitcast(FP8X4),
                    rhs_scale=plane[first_row:P, cols],
                    start=(g == 0),
                    stop=(g == PASSES - 1),
                )

        result = keep.tile([P, D_OUT], F32, name="result")
        out_rows = out.rearrange("b s d -> (b s) d")
        banks_per_chunk = BANKS // LAST_CHUNKS
        for c in range(LAST_CHUNKS):
            for j in range(c * banks_per_chunk, (c + 1) * banks_per_chunk):
                cols = slice(j * BANK, (j + 1) * BANK)
                if j % 2 == 0:
                    nc.vector.tensor_copy(out=result[:, cols], in_=acc[j][:])
                else:
                    nc.scalar.copy(out=result[:, cols], in_=acc[j][:])
            cols = slice(c * chunk, (c + 1) * chunk)
            nc.sync.dma_start(out=out_rows[:, cols], in_=result[:, cols])
